import numpy as np
import ml_dtypes


def mxq(x, axis, fmt="e4m3"):
    dtype, down = {"e4m3": (ml_dtypes.float8_e4m3fn, 7), "e5m2": (ml_dtypes.float8_e5m2, 14)}[fmt]
    v = np.moveaxis(np.asarray(x, np.float32).astype(ml_dtypes.bfloat16).astype(np.float64), axis, -1)
    blocks = v.reshape(v.shape[:-1] + (-1, 32))
    amax = np.abs(blocks).max(-1, keepdims=True)
    byte = np.maximum(np.where(amax > 0, np.frexp(amax)[1] - 1 + 127, 0) - down, 1)
    scale = np.exp2(byte - 127.0)
    codes = (blocks / scale).astype(np.float32).astype(dtype).astype(np.float64)
    return np.moveaxis((codes * scale).reshape(v.shape), -1, axis)


WIDE = False


def mx_kscale(k):
    if not WIDE:
        return np.ones(k)
    levels = np.array([10, -10, 5, -5, 0])
    a = np.random.permutation(np.resize(levels, k // 512 * 4)).reshape(k // 512, 4)
    idx = np.arange(k)
    return np.exp2(a[idx // 512, idx % 128 // 32])


BF16 = ml_dtypes.bfloat16


def bf(x):
    return np.asarray(x, np.float32).astype(BF16)


def f64(x):
    return np.asarray(x).astype(np.float64)


B, S, D, H, C = 1, 1024, 1024, 1024, 512


def setup_inputs():
    s, t = mx_kscale(H), mx_kscale(S)
    return {"q": bf(np.random.standard_normal((B, S, H)) * 0.6 * s),
            "k": bf(np.random.standard_normal((B, S, H)) * 0.6 / s * t[:, None]),
            "v": bf(np.random.standard_normal((B, S, H)) * 0.6 / t[:, None]),
            "decay": bf(np.random.uniform(0.5, 1.5, S) * 2.0 / S)}


def reference(q, k, v, decay):
    qq = mxq(f64(q), 2, "e4m3")
    kq = mxq(f64(k), 2, "e4m3")
    vq = mxq(f64(v), 1, "e4m3")
    idx = np.arange(S)
    diff = f64(np.abs(idx[None, :] - idx[:, None]))
    dm = np.exp(-f64(decay)[None, :] * diff) * np.tril(np.ones((S, S)))
    out = np.zeros((B, S, H))
    for r in range(0, S, C):
        e = r + C
        sc = (qq[:, r:e] @ kq[:, :e].transpose(0, 2, 1)) * dm[r:e, :e]
        sc = sc / np.sqrt(H)
        out[:, r:e] = mxq(sc, 2, "e4m3") @ vq[:, :e]
    return out

@@ -1,0 +1,212 @@
+from contextlib import ExitStack
+
+import concourse.mybir as mybir
+from concourse.masks import make_identity
+
+F32 = mybir.dt.float32
+BF16 = mybir.dt.bfloat16
+I32 = mybir.dt.int32
+U32 = mybir.dt.uint32
+U8 = mybir.dt.uint8
+FP8X4 = mybir.dt.float8_e4m3fn_x4
+ALU = mybir.AluOpType
+ACT = mybir.ActivationFunctionType
+
+P = 128
+S = 1024
+H = 1024
+CHUNK = 512
+TILES = CHUNK // P
+FLOPS = 2 * 2 * H * (CHUNK * CHUNK + CHUNK * 2 * CHUNK)
+
+VECTOR_FLIPS = (("k", 0, 0), ("k", 0, 1), ("k", 0, 2), ("k", 0, 3))
+VECTOR_OUTS = ((1, 2, 0), (1, 3, 0))
+
+
+def tile_simplifiedretnet_pa_kernel(tc, q, k, v, decay, out):
+    nc = tc.nc
+    q2 = q.rearrange("b s h -> (b s) h")
+    k2 = k.rearrange("b s h -> (b s) h")
+    v2 = v.rearrange("b s h -> (b s) h")
+    out2 = out.rearrange("b s h -> (b s) h")
+
+    with ExitStack() as stack:
+        keep = stack.enter_context(tc.tile_pool(name="keep", bufs=1))
+        tp = stack.enter_context(tc.psum_pool(name="tp", bufs=3))
+        sc = stack.enter_context(tc.psum_pool(name="sc", bufs=2))
+        ob = stack.enter_context(tc.psum_pool(name="ob", bufs=3))
+
+        dec = keep.tile([P, 2 * TILES], BF16, name="dec")
+        with nc.allow_non_contiguous_dma(reason="1024 decay rates, one key to a partition"):
+            nc.scalar.dma_start(
+                out=dec[:].rearrange("p (g t) -> p g t", g=2), in_=decay.rearrange("(g p t) -> p g t", g=2, t=TILES)
+            )
+
+        def load(src, chunk, name):
+            raw = keep.tile([P, TILES * H], BF16, name=name)
+            view = raw[:].rearrange("p (t h) -> p t h", t=TILES)
+            if name[4] == "q":
+                rows = src[CHUNK * chunk : CHUNK * (chunk + 1), :].rearrange("(t p) h -> p t h", p=P)
+            else:
+                rows = src[CHUNK * chunk : CHUNK * (chunk + 1), :].rearrange("(p t) h -> p t h", t=TILES)
+            for half in range(2):
+                nc.sync.dma_start(out=view[:, 2 * half : 2 * half + 2, :], in_=rows[:, 2 * half : 2 * half + 2, :])
+            return raw
+
+        raw = {}
+        for kind, src, chunk in (("k", k2, 0), ("q", q2, 0), ("v", v2, 0), ("q", q2, 1), ("k", k2, 1), ("v", v2, 1)):
+            raw[(kind, chunk)] = load(src, chunk, "raw_%s%d" % (kind, chunk))
+
+        warm = keep.tile([P, 1], F32, name="warm")
+        nc.vector.memset(warm[:], 0.0)
+        warm2 = keep.tile([P, 1], F32, name="warm2")
+        nc.scalar.activation(out=warm2[:], in_=warm[:], func=ACT.Exp)
+
+        ident = keep.tile([P, P], F32, name="ident")
+        make_identity(nc, ident[:])
+
+        ramp = keep.tile([P, 260], I32, name="ramp")
+        nc.gpsimd.iota(ramp[:], pattern=[[1, 260]], base=-3, channel_multiplier=-4)
+        dist = keep.tile([P, 1040], F32, name="dist")
+        for b in range(4):
+            nc.vector.tensor_scalar(
+                out=dist[:, 260 * b : 260 * (b + 1)], in0=ramp[:], scalar1=float(260 * b), scalar2=0.0,
+                op0=ALU.add, op1=ALU.max,
+            )
+        negd = keep.tile([P, 2 * TILES], F32, name="negd")
+        nc.vector.tensor_scalar_mul(out=negd[:], in0=dec[:], scalar1=-1.0)
+
+        s_grp = {}
+        for c in range(2):
+            for a in range(TILES):
+                s_grp[(c, a)] = keep.tile([P, (c + 1) * CHUNK], BF16, name="sg%d%d" % (c, a), align_bytes=64)
+
+        m_tab = {}
+
+        def decay_table(c, g):
+            m = keep.tile([P, TILES * CHUNK], F32, name="m%d%d" % (c, g))
+            m_tab[(c, g)] = m
+            for t in range(TILES):
+                i0 = 0
+                y0 = 3 - t + CHUNK * (c - g)
+                n = CHUNK
+                nc.scalar.activation(
+                    out=m[:, CHUNK * t + i0 : CHUNK * (t + 1)], in_=dist[:, y0 : y0 + n], func=ACT.Exp,
+                    scale=negd[:, TILES * g + t : TILES * g + t + 1],
+                )
+            if g == c:
+                for t in range(TILES):
+                    part = m[:, CHUNK * t : CHUNK * (t + 1)]
+                    nc.gpsimd.affine_select(
+                        out=part, in_=part, pattern=[[1, CHUNK]], compare_op=ALU.is_ge, fill=0.0,
+                        base=-t, channel_multiplier=-4,
+                    )
+
+        codes = {}
+        planes = {}
+
+        def flip(kind, chunk, t):
+            words = raw[(kind, chunk)][:].bitcast(F32)
+            bank = tp.tile([P, 512], F32, name="flip_bank")
+            for w in range(4):
+                nc.tensor.transpose(bank[:, P * w : P * (w + 1)], words[:, 512 * t + P * w : 512 * t + P * (w + 1)], ident[:])
+            grouped = keep.tile([P, H], BF16, name="g_%s%d%d" % (kind, chunk, t), align_bytes=64)
+            dst = grouped[:].bitcast(F32).rearrange("p (g r u) -> p g r u", g=2, u=2)
+            src = bank[:].rearrange("p (g u r) -> p g r u", g=2, u=2)
+            if (kind, chunk, t) in VECTOR_FLIPS:
+                nc.vector.tensor_copy(out=dst, in_=src)
+            else:
+                nc.scalar.copy(out=dst, in_=src)
+            return grouped
+
+        def quantise(key, grouped, width):
+            cd = keep.tile([P, width // 4], U32, name="c_%s" % key, align_bytes=64)
+            pl = keep.tile([P, width // 4], U8, name="p_%s" % key, align_bytes=64)
+            nc.vector.quantize_mx(out=cd[:].bitcast(FP8X4), scales=pl[:], in_=grouped[:])
+            codes[key] = cd
+            planes[key] = pl
+
+        def flip_chunk(kind, chunk):
+            gs = [flip(kind, chunk, t) for t in range(TILES)]
+            for t in range(TILES):
+                quantise("%s%d" % (kind, TILES * chunk + t), gs[t], H)
+
+        def values(g):
+            src_all = raw[("v", g)][:].rearrange("p (t h) -> p t h", t=TILES)
+            gs = []
+            for hh in range(2):
+                grouped = keep.tile([P, 4 * 512], BF16, name="g_v%d%d" % (g, hh), align_bytes=64)
+                nc.vector.tensor_copy(
+                    out=grouped[:].rearrange("p (c i t) -> p c t i", i=4, t=4),
+                    in_=src_all[:, :, 512 * hh : 512 * (hh + 1)].rearrange("p t (c i) -> p c t i", i=4),
+                )
+                gs.append(grouped)
+            for hh in range(2):
+                quantise("v%d%d" % (g, hh), gs[hh], 4 * 512)
+
+        def scores(c, g, a):
+            nt = TILES
+            bank = sc.tile([P, 512], F32, name="score_bank")
+            kq = "q%d" % (TILES * c + a)
+            for t in range(nt):
+                kk = "k%d" % (TILES * g + t)
+                for hp in range(2):
+                    cols = slice(P * hp, P * (hp + 1))
+                    nc.tensor.matmul_mx(
+                        out=bank[:, P * t : P * (t + 1)],
+                        lhsT=codes[kk][:, cols].bitcast(FP8X4), lhsT_scale=planes[kk][:, cols],
+                        rhs=codes[kq][:, cols].bitcast(FP8X4), rhs_scale=planes[kq][:, cols],
+                        start=(hp == 0), stop=(hp == 1),
+                    )
+            m = m_tab[(c, g)][:, 0 : TILES * CHUNK].rearrange("p (t i) -> p t i", t=TILES)
+            nc.vector.scalar_tensor_tensor(
+                out=s_grp[(c, a)][:, CHUNK * g : CHUNK * (g + 1)].rearrange("p (i t) -> p i t", t=TILES)[:, :, 0:nt],
+                in0=bank[:].rearrange("p (t i) -> p i t", t=TILES)[:, :, 0:nt],
+                scalar=1.0 / 32.0,
+                in1=m[:, 0:nt, P * a : P * (a + 1)].rearrange("p t i -> p i t"),
+                op0=ALU.mult, op1=ALU.mult,
+            )
+
+        def outputs(c, a):
+            ks = "s%d%d" % (c, a)
+            stage = keep.tile([P, H], F32, name="o%d%d" % (c, a))
+            for hh in range(2):
+                acc = ob.tile([P, 512], F32, name="out_bank")
+                for g in range(c + 1):
+                    cols = slice(P * g, P * (g + 1))
+                    kv = "v%d%d" % (g, hh)
+                    nc.tensor.matmul_mx(
+                        out=acc[:],
+                        lhsT=codes[ks][:, cols].bitcast(FP8X4), lhsT_scale=planes[ks][:, cols],
+                        rhs=codes[kv][:].bitcast(FP8X4), rhs_scale=planes[kv][:],
+                        start=(g == 0), stop=(g == c),
+                    )
+                if (c, a, hh) in VECTOR_OUTS:
+                    nc.vector.tensor_copy(out=stage[:, 512 * hh : 512 * (hh + 1)], in_=acc[:])
+                else:
+                    nc.scalar.copy(out=stage[:, 512 * hh : 512 * (hh + 1)], in_=acc[:])
+            row = CHUNK * c + P * a
+            nc.sync.dma_start(out=out2[row : row + P, :], in_=stage[:])
+
+        decay_table(0, 0)
+        flip_chunk("k", 0)
+        flip_chunk("q", 0)
+        for a in range(TILES):
+            scores(0, 0, a)
+        for a in range(TILES):
+            quantise("s0%d" % a, s_grp[(0, a)], CHUNK)
+        values(0)
+        decay_table(1, 0)
+        decay_table(1, 1)
+        for a in range(TILES):
+            outputs(0, a)
+        flip_chunk("q", 1)
+        for a in range(TILES):
+            scores(1, 0, a)
+        flip_chunk("k", 1)
+        for a in range(TILES):
+            scores(1, 1, a)
+            quantise("s1%d" % a, s_grp[(1, a)], 2 * CHUNK)
+        values(1)
+        for a in range(TILES):
+            outputs(1, a)

@@ -17,54 +17,153 @@ S = 1024
 H = 1024
 CHUNK = 512
 TILES = CHUNK // P
+BANK = 512
 FLOPS = 2 * 2 * H * (CHUNK * CHUNK + CHUNK * 2 * CHUNK)
-
-VECTOR_FLIPS = (("k", 0, 0), ("k", 0, 1), ("k", 0, 2), ("k", 0, 3))
-VECTOR_OUTS = ((1, 2, 0), (1, 3, 0))
 
 
 def tile_simplifiedretnet_pa_kernel(tc, q, k, v, decay, out):
     nc = tc.nc
-    q2 = q.rearrange("b s h -> (b s) h")
-    k2 = k.rearrange("b s h -> (b s) h")
-    v2 = v.rearrange("b s h -> (b s) h")
+    dram = {
+        "q": q.rearrange("b s h -> (b s) h"),
+        "k": k.rearrange("b s h -> (b s) h"),
+        "v": v.rearrange("b s h -> (b s) h"),
+    }
     out2 = out.rearrange("b s h -> (b s) h")
 
     with ExitStack() as stack:
         keep = stack.enter_context(tc.tile_pool(name="keep", bufs=1))
-        tp = stack.enter_context(tc.psum_pool(name="tp", bufs=3))
-        sc = stack.enter_context(tc.psum_pool(name="sc", bufs=2))
-        ob = stack.enter_context(tc.psum_pool(name="ob", bufs=3))
+        psum = stack.enter_context(tc.psum_pool(name="psum", bufs=8))
+        stack.enter_context(tc.manual_schedule())
+
+        raw = {}
+        grouped = {}
+        banks = {}
+        codes = {}
+        planes = {}
+        tables = {}
+        stages = {}
+
+        def load(kind, chunk):
+            tile_ = keep.tile([P, TILES * H], BF16, name="raw_%s%d" % (kind, chunk))
+            raw[(kind, chunk)] = tile_
+            view = tile_[:].rearrange("p (t h) -> p t h", t=TILES)
+            rows = dram[kind][CHUNK * chunk : CHUNK * (chunk + 1), :]
+            if kind == "q":
+                rows = rows.rearrange("(t p) h -> p t h", p=P)
+            else:
+                rows = rows.rearrange("(p t) h -> p t h", t=TILES)
+            for half in range(2):
+                nc.sync.dma_start(out=view[:, 2 * half : 2 * half + 2, :], in_=rows[:, 2 * half : 2 * half + 2, :])
+
+        def table_exp(c, g, t):
+            if t == 0:
+                tables[(c, g)] = keep.tile([P, TILES * CHUNK], F32, name="m%d%d" % (c, g))
+            y0 = 3 - t + CHUNK * (c - g)
+            part = tables[(c, g)][:, CHUNK * t : CHUNK * (t + 1)]
+            nc.scalar.activation(
+                out=part, in_=dist[:, y0 : y0 + CHUNK], func=ACT.Exp, scale=negd[:, TILES * g + t : TILES * g + t + 1]
+            )
+            if g == c:
+                nc.gpsimd.affine_select(
+                    out=part, in_=part, pattern=[[1, CHUNK]], compare_op=ALU.is_ge, fill=0.0, base=-t, channel_multiplier=-4
+                )
+
+        def transposes(kind, n):
+            words = raw[(kind, n // TILES)][:].bitcast(F32)
+            bank = psum.tile([P, BANK], F32, name="bank")
+            banks[(kind, n)] = bank
+            first = BANK * (n % TILES)
+            for w in range(4):
+                nc.tensor.transpose(bank[:, P * w : P * (w + 1)], words[:, first + P * w : first + P * (w + 1)], ident[:])
+
+        def regroup(kind, n, engine):
+            tile_ = keep.tile([P, H], BF16, name="g_%s%d" % (kind, n), align_bytes=64)
+            grouped[(kind, n)] = tile_
+            dst = tile_[:].bitcast(F32).rearrange("p (g r u) -> p g r u", g=2, u=2)
+            src = banks[(kind, n)][:].rearrange("p (g u r) -> p g r u", g=2, u=2)
+            if engine == "vector":
+                nc.vector.tensor_copy(out=dst, in_=src)
+            else:
+                nc.scalar.copy(out=dst, in_=src)
+
+        def quantise(kind, n):
+            width = grouped[(kind, n)].shape[1]
+            cd = keep.tile([P, width // 4], U32, name="c_%s%d" % (kind, n), align_bytes=64)
+            pl = keep.tile([P, width // 4], U8, name="p_%s%d" % (kind, n), align_bytes=64)
+            nc.vector.quantize_mx(out=cd[:].bitcast(FP8X4), scales=pl[:], in_=grouped[(kind, n)][:])
+            codes[(kind, n)] = cd
+            planes[(kind, n)] = pl
+
+        def regroup_values(g, hh):
+            tile_ = keep.tile([P, 4 * BANK], BF16, name="g_v%d%d" % (g, hh), align_bytes=64)
+            grouped[("v", 2 * g + hh)] = tile_
+            src = raw[("v", g)][:].rearrange("p (t h) -> p t h", t=TILES)[:, :, BANK * hh : BANK * (hh + 1)]
+            nc.vector.tensor_copy(
+                out=tile_[:].rearrange("p (c i t) -> p c t i", i=4, t=4), in_=src.rearrange("p t (c i) -> p c t i", i=4)
+            )
+
+        def mx(dst, left, lcols, right, rcols, start, stop):
+            nc.tensor.matmul_mx(
+                out=dst,
+                lhsT=codes[left][:, lcols].bitcast(FP8X4), lhsT_scale=planes[left][:, lcols],
+                rhs=codes[right][:, rcols].bitcast(FP8X4), rhs_scale=planes[right][:, rcols],
+                start=start, stop=stop,
+            )
+
+        def score_passes(c, g, a):
+            bank = psum.tile([P, BANK], F32, name="bank")
+            banks[("s", c, g, a)] = bank
+            for t in range(TILES):
+                for hp in range(2):
+                    cols = slice(P * hp, P * (hp + 1))
+                    mx(bank[:, P * t : P * (t + 1)], ("k", TILES * g + t), cols, ("q", TILES * c + a), cols, hp == 0, hp == 1)
+
+        def weigh(c, g, a):
+            n = TILES * c + a
+            if g == 0:
+                grouped[("s", n)] = keep.tile([P, (c + 1) * CHUNK], BF16, name="g_s%d" % n, align_bytes=64)
+            m = tables[(c, g)][:].rearrange("p (t i) -> p t i", t=TILES)
+            nc.vector.scalar_tensor_tensor(
+                out=grouped[("s", n)][:, CHUNK * g : CHUNK * (g + 1)].rearrange("p (i t) -> p i t", t=TILES),
+                in0=banks[("s", c, g, a)][:].rearrange("p (t i) -> p i t", t=TILES),
+                scalar=1.0 / 32.0,
+                in1=m[:, :, P * a : P * (a + 1)].rearrange("p t i -> p i t"),
+                op0=ALU.mult, op1=ALU.mult,
+            )
+
+        def output_passes(c, a, hh):
+            acc = psum.tile([P, BANK], F32, name="bank")
+            banks[("o", c, a, hh)] = acc
+            for g in range(c + 1):
+                mx(acc[:], ("s", TILES * c + a), slice(P * g, P * (g + 1)), ("v", 2 * g + hh), slice(0, BANK), g == 0, g == c)
+
+        def empty(c, a, hh, engine):
+            if hh == 0:
+                stages[(c, a)] = keep.tile([P, H], F32, name="o%d%d" % (c, a))
+            dst = stages[(c, a)][:, BANK * hh : BANK * (hh + 1)]
+            if engine == "vector":
+                nc.vector.tensor_copy(out=dst, in_=banks[("o", c, a, hh)][:])
+            else:
+                nc.scalar.copy(out=dst, in_=banks[("o", c, a, hh)][:])
+
+        def store(c, a):
+            row = CHUNK * c + P * a
+            nc.sync.dma_start(out=out2[row : row + P, :], in_=stages[(c, a)][:])
 
         dec = keep.tile([P, 2 * TILES], BF16, name="dec")
-        with nc.allow_non_contiguous_dma(reason="1024 decay rates, one key to a partition"):
+        with nc.allow_non_contiguous_dma(reason="1024 decay rates, four neighbouring keys to a partition"):
             nc.scalar.dma_start(
                 out=dec[:].rearrange("p (g t) -> p g t", g=2), in_=decay.rearrange("(g p t) -> p g t", g=2, t=TILES)
             )
-
-        def load(src, chunk, name):
-            raw = keep.tile([P, TILES * H], BF16, name=name)
-            view = raw[:].rearrange("p (t h) -> p t h", t=TILES)
-            if name[4] == "q":
-                rows = src[CHUNK * chunk : CHUNK * (chunk + 1), :].rearrange("(t p) h -> p t h", p=P)
-            else:
-                rows = src[CHUNK * chunk : CHUNK * (chunk + 1), :].rearrange("(p t) h -> p t h", t=TILES)
-            for half in range(2):
-                nc.sync.dma_start(out=view[:, 2 * half : 2 * half + 2, :], in_=rows[:, 2 * half : 2 * half + 2, :])
-            return raw
-
-        raw = {}
-        for kind, src, chunk in (("k", k2, 0), ("q", q2, 0), ("v", v2, 0), ("q", q2, 1), ("k", k2, 1), ("v", v2, 1)):
-            raw[(kind, chunk)] = load(src, chunk, "raw_%s%d" % (kind, chunk))
+        for kind, chunk in (("k", 0), ("q", 0), ("v", 0), ("q", 1), ("k", 1), ("v", 1)):
+            load(kind, chunk)
 
         warm = keep.tile([P, 1], F32, name="warm")
         nc.vector.memset(warm[:], 0.0)
         warm2 = keep.tile([P, 1], F32, name="warm2")
         nc.scalar.activation(out=warm2[:], in_=warm[:], func=ACT.Exp)
-
         ident = keep.tile([P, P], F32, name="ident")
         make_identity(nc, ident[:])
-
         ramp = keep.tile([P, 260], I32, name="ramp")
         nc.gpsimd.iota(ramp[:], pattern=[[1, 260]], base=-3, channel_multiplier=-4)
         dist = keep.tile([P, 1040], F32, name="dist")
@@ -76,137 +175,60 @@ def tile_simplifiedretnet_pa_kernel(tc, q, k, v, decay, out):
         negd = keep.tile([P, 2 * TILES], F32, name="negd")
         nc.vector.tensor_scalar_mul(out=negd[:], in0=dec[:], scalar1=-1.0)
 
-        s_grp = {}
-        for c in range(2):
+        for t in range(TILES):
+            table_exp(0, 0, t)
+        for t in range(TILES):
+            transposes("k", t)
+            regroup("k", t, "vector")
+            if t > 0:
+                quantise("k", t - 1)
+        quantise("k", TILES - 1)
+        for a in range(TILES):
+            transposes("q", a)
+            regroup("q", a, "scalar")
+        for a in range(TILES):
+            quantise("q", a)
+        for t in range(TILES):
+            table_exp(1, 0, t)
+        for a in range(TILES):
+            score_passes(0, 0, a)
+            weigh(0, 0, a)
+            if a > 0:
+                quantise("s", a - 1)
+        quantise("s", TILES - 1)
+        for hh in range(2):
+            regroup_values(0, hh)
+        for hh in range(2):
+            quantise("v", hh)
+
+        for kind in ("q", "k"):
             for a in range(TILES):
-                s_grp[(c, a)] = keep.tile([P, (c + 1) * CHUNK], BF16, name="sg%d%d" % (c, a), align_bytes=64)
+                transposes(kind, TILES + a)
+                regroup(kind, TILES + a, "scalar")
+        for t in range(TILES):
+            table_exp(1, 1, t)
+        for a in range(TILES):
+            quantise("q", TILES + a)
 
-        m_tab = {}
-
-        def decay_table(c, g):
-            m = keep.tile([P, TILES * CHUNK], F32, name="m%d%d" % (c, g))
-            m_tab[(c, g)] = m
-            for t in range(TILES):
-                i0 = 0
-                y0 = 3 - t + CHUNK * (c - g)
-                n = CHUNK
-                nc.scalar.activation(
-                    out=m[:, CHUNK * t + i0 : CHUNK * (t + 1)], in_=dist[:, y0 : y0 + n], func=ACT.Exp,
-                    scale=negd[:, TILES * g + t : TILES * g + t + 1],
-                )
-            if g == c:
-                for t in range(TILES):
-                    part = m[:, CHUNK * t : CHUNK * (t + 1)]
-                    nc.gpsimd.affine_select(
-                        out=part, in_=part, pattern=[[1, CHUNK]], compare_op=ALU.is_ge, fill=0.0,
-                        base=-t, channel_multiplier=-4,
-                    )
-
-        codes = {}
-        planes = {}
-
-        def flip(kind, chunk, t):
-            words = raw[(kind, chunk)][:].bitcast(F32)
-            bank = tp.tile([P, 512], F32, name="flip_bank")
-            for w in range(4):
-                nc.tensor.transpose(bank[:, P * w : P * (w + 1)], words[:, 512 * t + P * w : 512 * t + P * (w + 1)], ident[:])
-            grouped = keep.tile([P, H], BF16, name="g_%s%d%d" % (kind, chunk, t), align_bytes=64)
-            dst = grouped[:].bitcast(F32).rearrange("p (g r u) -> p g r u", g=2, u=2)
-            src = bank[:].rearrange("p (g u r) -> p g r u", g=2, u=2)
-            if (kind, chunk, t) in VECTOR_FLIPS:
-                nc.vector.tensor_copy(out=dst, in_=src)
-            else:
-                nc.scalar.copy(out=dst, in_=src)
-            return grouped
-
-        def quantise(key, grouped, width):
-            cd = keep.tile([P, width // 4], U32, name="c_%s" % key, align_bytes=64)
-            pl = keep.tile([P, width // 4], U8, name="p_%s" % key, align_bytes=64)
-            nc.vector.quantize_mx(out=cd[:].bitcast(FP8X4), scales=pl[:], in_=grouped[:])
-            codes[key] = cd
-            planes[key] = pl
-
-        def flip_chunk(kind, chunk):
-            gs = [flip(kind, chunk, t) for t in range(TILES)]
-            for t in range(TILES):
-                quantise("%s%d" % (kind, TILES * chunk + t), gs[t], H)
-
-        def values(g):
-            src_all = raw[("v", g)][:].rearrange("p (t h) -> p t h", t=TILES)
-            gs = []
+        for a in range(TILES):
+            score_passes(1, 0, a)
+            weigh(1, 0, a)
+            quantise("k", TILES + a)
             for hh in range(2):
-                grouped = keep.tile([P, 4 * 512], BF16, name="g_v%d%d" % (g, hh), align_bytes=64)
-                nc.vector.tensor_copy(
-                    out=grouped[:].rearrange("p (c i t) -> p c t i", i=4, t=4),
-                    in_=src_all[:, :, 512 * hh : 512 * (hh + 1)].rearrange("p t (c i) -> p c t i", i=4),
-                )
-                gs.append(grouped)
+                output_passes(0, a, hh)
+                empty(0, a, hh, "scalar")
+            store(0, a)
+        for hh in range(2):
+            regroup_values(1, hh)
+        for hh in range(2):
+            quantise("v", 2 + hh)
+
+        for a in range(TILES):
+            score_passes(1, 1, a)
+        for a in range(TILES):
+            weigh(1, 1, a)
+            quantise("s", TILES + a)
             for hh in range(2):
-                quantise("v%d%d" % (g, hh), gs[hh], 4 * 512)
-
-        def scores(c, g, a):
-            nt = TILES
-            bank = sc.tile([P, 512], F32, name="score_bank")
-            kq = "q%d" % (TILES * c + a)
-            for t in range(nt):
-                kk = "k%d" % (TILES * g + t)
-                for hp in range(2):
-                    cols = slice(P * hp, P * (hp + 1))
-                    nc.tensor.matmul_mx(
-                        out=bank[:, P * t : P * (t + 1)],
-                        lhsT=codes[kk][:, cols].bitcast(FP8X4), lhsT_scale=planes[kk][:, cols],
-                        rhs=codes[kq][:, cols].bitcast(FP8X4), rhs_scale=planes[kq][:, cols],
-                        start=(hp == 0), stop=(hp == 1),
-                    )
-            m = m_tab[(c, g)][:, 0 : TILES * CHUNK].rearrange("p (t i) -> p t i", t=TILES)
-            nc.vector.scalar_tensor_tensor(
-                out=s_grp[(c, a)][:, CHUNK * g : CHUNK * (g + 1)].rearrange("p (i t) -> p i t", t=TILES)[:, :, 0:nt],
-                in0=bank[:].rearrange("p (t i) -> p i t", t=TILES)[:, :, 0:nt],
-                scalar=1.0 / 32.0,
-                in1=m[:, 0:nt, P * a : P * (a + 1)].rearrange("p t i -> p i t"),
-                op0=ALU.mult, op1=ALU.mult,
-            )
-
-        def outputs(c, a):
-            ks = "s%d%d" % (c, a)
-            stage = keep.tile([P, H], F32, name="o%d%d" % (c, a))
-            for hh in range(2):
-                acc = ob.tile([P, 512], F32, name="out_bank")
-                for g in range(c + 1):
-                    cols = slice(P * g, P * (g + 1))
-                    kv = "v%d%d" % (g, hh)
-                    nc.tensor.matmul_mx(
-                        out=acc[:],
-                        lhsT=codes[ks][:, cols].bitcast(FP8X4), lhsT_scale=planes[ks][:, cols],
-                        rhs=codes[kv][:].bitcast(FP8X4), rhs_scale=planes[kv][:],
-                        start=(g == 0), stop=(g == c),
-                    )
-                if (c, a, hh) in VECTOR_OUTS:
-                    nc.vector.tensor_copy(out=stage[:, 512 * hh : 512 * (hh + 1)], in_=acc[:])
-                else:
-                    nc.scalar.copy(out=stage[:, 512 * hh : 512 * (hh + 1)], in_=acc[:])
-            row = CHUNK * c + P * a
-            nc.sync.dma_start(out=out2[row : row + P, :], in_=stage[:])
-
-        decay_table(0, 0)
-        flip_chunk("k", 0)
-        flip_chunk("q", 0)
-        for a in range(TILES):
-            scores(0, 0, a)
-        for a in range(TILES):
-            quantise("s0%d" % a, s_grp[(0, a)], CHUNK)
-        values(0)
-        decay_table(1, 0)
-        decay_table(1, 1)
-        for a in range(TILES):
-            outputs(0, a)
-        flip_chunk("q", 1)
-        for a in range(TILES):
-            scores(1, 0, a)
-        flip_chunk("k", 1)
-        for a in range(TILES):
-            scores(1, 1, a)
-            quantise("s1%d" % a, s_grp[(1, a)], 2 * CHUNK)
-        values(1)
-        for a in range(TILES):
-            outputs(1, a)
+                output_passes(1, a, hh)
+                empty(1, a, hh, "vector" if (a == TILES - 1 and hh == 0) else "scalar")
+            store(1, a)

@@ -43,44 +43,41 @@ def tile_simplifiedretnet_pa_kernel(tc, q, k, v, decay, out):
         tables = {}
         stages = {}
 
-        def load(kind, chunk):
-            tile_ = keep.tile([P, TILES * H], BF16, name="raw_%s%d" % (kind, chunk))
-            raw[(kind, chunk)] = tile_
-            view = tile_[:].rearrange("p (t h) -> p t h", t=TILES)
-            rows = dram[kind][CHUNK * chunk : CHUNK * (chunk + 1), :]
-            if kind == "q":
-                rows = rows.rearrange("(t p) h -> p t h", p=P)
-            else:
-                rows = rows.rearrange("(p t) h -> p t h", t=TILES)
+        def load_rows(kind, n):
+            raw[(kind, n)] = keep.tile([P, H], BF16, name="raw_%s%d" % (kind, n))
+            nc.sync.dma_start(out=raw[(kind, n)][:], in_=dram[kind][P * n : P * (n + 1), :])
+
+        def load_values(g):
+            raw[("v", g)] = keep.tile([P, TILES * H], BF16, name="raw_v%d" % g)
+            view = raw[("v", g)][:].rearrange("p (t h) -> p t h", t=TILES)
+            rows = dram["v"][CHUNK * g : CHUNK * (g + 1), :].rearrange("(t p) h -> p t h", p=P)
             for half in range(2):
                 nc.sync.dma_start(out=view[:, 2 * half : 2 * half + 2, :], in_=rows[:, 2 * half : 2 * half + 2, :])
 
-        def table_exp(c, g, t):
-            if t == 0:
+        def table(c, g, t):
+            if (c, g) not in tables:
                 tables[(c, g)] = keep.tile([P, TILES * CHUNK], F32, name="m%d%d" % (c, g))
-            y0 = 3 - t + CHUNK * (c - g)
-            part = tables[(c, g)][:, CHUNK * t : CHUNK * (t + 1)]
+            i0 = P * t if g == c else 0
+            y0 = 0 if g == c else CHUNK - P * t
+            m = tables[(c, g)]
             nc.scalar.activation(
-                out=part, in_=dist[:, y0 : y0 + CHUNK], func=ACT.Exp, scale=negd[:, TILES * g + t : TILES * g + t + 1]
+                out=m[:, CHUNK * t + i0 : CHUNK * (t + 1)], in_=dist[:, y0 : y0 + CHUNK - i0], func=ACT.Exp,
+                scale=negd[:, TILES * g + t : TILES * g + t + 1],
             )
             if g == c:
+                corner = m[:, CHUNK * t + i0 : CHUNK * t + i0 + P]
                 nc.gpsimd.affine_select(
-                    out=part, in_=part, pattern=[[1, CHUNK]], compare_op=ALU.is_ge, fill=0.0, base=-t, channel_multiplier=-4
+                    out=corner, in_=corner, pattern=[[1, P]], compare_op=ALU.is_ge, fill=0.0, base=0, channel_multiplier=-1
                 )
 
-        def transposes(kind, n):
-            words = raw[(kind, n // TILES)][:].bitcast(F32)
+        def flip(kind, n, engine):
+            words = raw[(kind, n)][:].bitcast(F32)
             bank = psum.tile([P, BANK], F32, name="bank")
-            banks[(kind, n)] = bank
-            first = BANK * (n % TILES)
             for w in range(4):
-                nc.tensor.transpose(bank[:, P * w : P * (w + 1)], words[:, first + P * w : first + P * (w + 1)], ident[:])
-
-        def regroup(kind, n, engine):
-            tile_ = keep.tile([P, H], BF16, name="g_%s%d" % (kind, n), align_bytes=64)
-            grouped[(kind, n)] = tile_
-            dst = tile_[:].bitcast(F32).rearrange("p (g r u) -> p g r u", g=2, u=2)
-            src = banks[(kind, n)][:].rearrange("p (g u r) -> p g r u", g=2, u=2)
+                nc.tensor.transpose(bank[:, P * w : P * (w + 1)], words[:, P * w : P * (w + 1)], ident[:])
+            grouped[(kind, n)] = keep.tile([P, H], BF16, name="g_%s%d" % (kind, n), align_bytes=64)
+            dst = grouped[(kind, n)][:].bitcast(F32).rearrange("p (g r u) -> p g r u", g=2, u=2)
+            src = bank[:].rearrange("p (g u r) -> p g r u", g=2, u=2)
             if engine == "vector":
                 nc.vector.tensor_copy(out=dst, in_=src)
             else:
@@ -95,11 +92,11 @@ def tile_simplifiedretnet_pa_kernel(tc, q, k, v, decay, out):
             planes[(kind, n)] = pl
 
         def regroup_values(g, hh):
-            tile_ = keep.tile([P, 4 * BANK], BF16, name="g_v%d%d" % (g, hh), align_bytes=64)
-            grouped[("v", 2 * g + hh)] = tile_
+            grouped[("v", 2 * g + hh)] = keep.tile([P, 4 * BANK], BF16, name="g_v%d%d" % (g, hh), align_bytes=64)
             src = raw[("v", g)][:].rearrange("p (t h) -> p t h", t=TILES)[:, :, BANK * hh : BANK * (hh + 1)]
             nc.vector.tensor_copy(
-                out=tile_[:].rearrange("p (c i t) -> p c t i", i=4, t=4), in_=src.rearrange("p t (c i) -> p c t i", i=4)
+                out=grouped[("v", 2 * g + hh)][:].rearrange("p (c i t) -> p c t i", i=4, t=4),
+                in_=src.rearrange("p t (c i) -> p c t i", i=4),
             )
 
         def mx(dst, left, lcols, right, rcols, start, stop):
@@ -110,53 +107,46 @@ def tile_simplifiedretnet_pa_kernel(tc, q, k, v, decay, out):
                 start=start, stop=stop,
             )
 
-        def score_passes(c, g, a):
+        def scores(c, g, a):
+            nt = TILES if g < c else a + 1
             bank = psum.tile([P, BANK], F32, name="bank")
-            banks[("s", c, g, a)] = bank
-            for t in range(TILES):
+            for t in range(nt):
                 for hp in range(2):
                     cols = slice(P * hp, P * (hp + 1))
                     mx(bank[:, P * t : P * (t + 1)], ("k", TILES * g + t), cols, ("q", TILES * c + a), cols, hp == 0, hp == 1)
-
-        def weigh(c, g, a):
-            n = TILES * c + a
-            if g == 0:
-                grouped[("s", n)] = keep.tile([P, (c + 1) * CHUNK], BF16, name="g_s%d" % n, align_bytes=64)
             m = tables[(c, g)][:].rearrange("p (t i) -> p t i", t=TILES)
+            part = grouped[("s", TILES * c + a)][:, CHUNK * g : CHUNK * (g + 1)]
             nc.vector.scalar_tensor_tensor(
-                out=grouped[("s", n)][:, CHUNK * g : CHUNK * (g + 1)].rearrange("p (i t) -> p i t", t=TILES),
-                in0=banks[("s", c, g, a)][:].rearrange("p (t i) -> p i t", t=TILES),
+                out=part.rearrange("p (i t) -> p i t", t=TILES)[:, :, 0:nt],
+                in0=bank[:].rearrange("p (t i) -> p i t", t=TILES)[:, :, 0:nt],
                 scalar=1.0 / 32.0,
-                in1=m[:, :, P * a : P * (a + 1)].rearrange("p t i -> p i t"),
+                in1=m[:, 0:nt, P * a : P * (a + 1)].rearrange("p t i -> p i t"),
                 op0=ALU.mult, op1=ALU.mult,
             )
 
-        def output_passes(c, a, hh):
+        def outputs(c, a, hh, engine):
             acc = psum.tile([P, BANK], F32, name="bank")
-            banks[("o", c, a, hh)] = acc
             for g in range(c + 1):
                 mx(acc[:], ("s", TILES * c + a), slice(P * g, P * (g + 1)), ("v", 2 * g + hh), slice(0, BANK), g == 0, g == c)
-
-        def empty(c, a, hh, engine):
-            if hh == 0:
-                stages[(c, a)] = keep.tile([P, H], F32, name="o%d%d" % (c, a))
-            dst = stages[(c, a)][:, BANK * hh : BANK * (hh + 1)]
+            stages[(c, a, hh)] = keep.tile([P, BANK], F32, name="o%d%d%d" % (c, a, hh))
             if engine == "vector":
-                nc.vector.tensor_copy(out=dst, in_=banks[("o", c, a, hh)][:])
+                nc.vector.tensor_copy(out=stages[(c, a, hh)][:], in_=acc[:])
             else:
-                nc.scalar.copy(out=dst, in_=banks[("o", c, a, hh)][:])
-
-        def store(c, a):
+                nc.scalar.copy(out=stages[(c, a, hh)][:], in_=acc[:])
             row = CHUNK * c + P * a
-            nc.sync.dma_start(out=out2[row : row + P, :], in_=stages[(c, a)][:])
+            nc.sync.dma_start(out=out2[row : row + P, BANK * hh : BANK * (hh + 1)], in_=stages[(c, a, hh)][:])
 
         dec = keep.tile([P, 2 * TILES], BF16, name="dec")
-        with nc.allow_non_contiguous_dma(reason="1024 decay rates, four neighbouring keys to a partition"):
-            nc.scalar.dma_start(
-                out=dec[:].rearrange("p (g t) -> p g t", g=2), in_=decay.rearrange("(g p t) -> p g t", g=2, t=TILES)
-            )
-        for kind, chunk in (("k", 0), ("q", 0), ("v", 0), ("q", 1), ("k", 1), ("v", 1)):
-            load(kind, chunk)
+        with nc.allow_non_contiguous_dma(reason="1024 decay rates, one key to a partition"):
+            nc.scalar.dma_start(out=dec[:], in_=decay.rearrange("(t p) -> p t", p=P))
+        for n in range(TILES):
+            load_rows("k", n)
+            load_rows("q", n)
+        load_values(0)
+        for n in range(TILES, 2 * TILES):
+            load_rows("q", n)
+            load_rows("k", n)
+        load_values(1)
 
         warm = keep.tile([P, 1], F32, name="warm")
         nc.vector.memset(warm[:], 0.0)
@@ -164,71 +154,104 @@ def tile_simplifiedretnet_pa_kernel(tc, q, k, v, decay, out):
         nc.scalar.activation(out=warm2[:], in_=warm[:], func=ACT.Exp)
         ident = keep.tile([P, P], F32, name="ident")
         make_identity(nc, ident[:])
-        ramp = keep.tile([P, 260], I32, name="ramp")
-        nc.gpsimd.iota(ramp[:], pattern=[[1, 260]], base=-3, channel_multiplier=-4)
-        dist = keep.tile([P, 1040], F32, name="dist")
+        ramp = keep.tile([P, 256], I32, name="ramp")
+        nc.gpsimd.iota(ramp[:], pattern=[[1, 256]], base=0, channel_multiplier=-1)
+        for c in range(2):
+            for a in range(TILES):
+                n = TILES * c + a
+                grouped[("s", n)] = keep.tile([P, (c + 1) * CHUNK], BF16, name="g_s%d" % n, align_bytes=64)
+                if a < TILES - 1:
+                    nc.vector.memset(grouped[("s", n)][:, c * CHUNK : (c + 1) * CHUNK], 0.0)
+        dist = keep.tile([P, S], F32, name="dist")
         for b in range(4):
             nc.vector.tensor_scalar(
-                out=dist[:, 260 * b : 260 * (b + 1)], in0=ramp[:], scalar1=float(260 * b), scalar2=0.0,
+                out=dist[:, 256 * b : 256 * (b + 1)], in0=ramp[:], scalar1=float(256 * b), scalar2=0.0,
                 op0=ALU.add, op1=ALU.max,
             )
         negd = keep.tile([P, 2 * TILES], F32, name="negd")
         nc.vector.tensor_scalar_mul(out=negd[:], in0=dec[:], scalar1=-1.0)
 
-        for t in range(TILES):
-            table_exp(0, 0, t)
-        for t in range(TILES):
-            transposes("k", t)
-            regroup("k", t, "vector")
-            if t > 0:
-                quantise("k", t - 1)
-        quantise("k", TILES - 1)
-        for a in range(TILES):
-            transposes("q", a)
-            regroup("q", a, "scalar")
-        for a in range(TILES):
-            quantise("q", a)
-        for t in range(TILES):
-            table_exp(1, 0, t)
-        for a in range(TILES):
-            score_passes(0, 0, a)
-            weigh(0, 0, a)
-            if a > 0:
-                quantise("s", a - 1)
-        quantise("s", TILES - 1)
-        for hh in range(2):
-            regroup_values(0, hh)
-        for hh in range(2):
-            quantise("v", hh)
+        flip("k", 0, "vector")
+        table(0, 0, 0)
+        table(0, 0, 1)
+        flip("q", 0, "vector")
+        flip("k", 1, "vector")
+        table(0, 0, 2)
+        flip("q", 1, "scalar")
+        for n in range(2):
+            quantise("k", n)
+            quantise("q", n)
+        flip("k", 2, "scalar")
+        flip("q", 2, "scalar")
+        scores(0, 0, 0)
+        quantise("k", 2)
+        quantise("q", 2)
+        flip("k", 3, "scalar")
+        flip("q", 3, "scalar")
+        table(0, 0, 3)
+        scores(0, 0, 1)
+        quantise("s", 0)
+        quantise("k", 3)
+        quantise("q", 3)
+        scores(0, 0, 2)
+        quantise("s", 1)
+        table(1, 0, 0)
+        table(1, 0, 1)
+        regroup_values(0, 0)
+        scores(0, 0, 3)
+        regroup_values(0, 1)
+        for n in (4, 5):
+            flip("q", n, "scalar")
+            flip("k", n, "scalar")
+        quantise("s", 2)
+        quantise("v", 0)
+        quantise("s", 3)
+        quantise("v", 1)
+        table(1, 0, 2)
+        table(1, 0, 3)
+        table(1, 1, 0)
+        for n in (4, 5):
+            quantise("q", n)
+            quantise("k", n)
 
-        for kind in ("q", "k"):
-            for a in range(TILES):
-                transposes(kind, TILES + a)
-                regroup(kind, TILES + a, "scalar")
-        for t in range(TILES):
-            table_exp(1, 1, t)
-        for a in range(TILES):
-            quantise("q", TILES + a)
-
-        for a in range(TILES):
-            score_passes(1, 0, a)
-            weigh(1, 0, a)
-            quantise("k", TILES + a)
-            for hh in range(2):
-                output_passes(0, a, hh)
-                empty(0, a, hh, "scalar")
-            store(0, a)
-        for hh in range(2):
-            regroup_values(1, hh)
-        for hh in range(2):
-            quantise("v", 2 + hh)
-
-        for a in range(TILES):
-            score_passes(1, 1, a)
-        for a in range(TILES):
-            weigh(1, 1, a)
-            quantise("s", TILES + a)
-            for hh in range(2):
-                output_passes(1, a, hh)
-                empty(1, a, hh, "vector" if (a == TILES - 1 and hh == 0) else "scalar")
-            store(1, a)
+        outputs(0, 0, 0, "scalar")
+        outputs(0, 0, 1, "scalar")
+        scores(1, 0, 0)
+        scores(1, 1, 0)
+        outputs(0, 1, 0, "scalar")
+        outputs(0, 1, 1, "scalar")
+        regroup_values(1, 0)
+        regroup_values(1, 1)
+        for n in (6, 7):
+            flip("q", n, "scalar")
+            flip("k", n, "scalar")
+        table(1, 1, 1)
+        quantise("s", 4)
+        for n in (6, 7):
+            quantise("q", n)
+            quantise("k", n)
+        quantise("v", 2)
+        quantise("v", 3)
+        outputs(0, 2, 0, "scalar")
+        outputs(0, 2, 1, "scalar")
+        scores(1, 0, 1)
+        scores(1, 1, 1)
+        outputs(0, 3, 0, "scalar")
+        outputs(0, 3, 1, "scalar")
+        table(1, 1, 2)
+        table(1, 1, 3)
+        quantise("s", 5)
+        scores(1, 0, 2)
+        scores(1, 1, 2)
+        quantise("s", 6)
+        outputs(1, 0, 0, "scalar")
+        outputs(1, 0, 1, "scalar")
+        scores(1, 0, 3)
+        scores(1, 1, 3)
+        quantise("s", 7)
+        outputs(1, 1, 0, "scalar")
+        outputs(1, 1, 1, "scalar")
+        outputs(1, 2, 0, "scalar")
+        outputs(1, 2, 1, "vector")
+        outputs(1, 3, 0, "vector")
+        outputs(1, 3, 1, "scalar")

@@ -240,17 +240,17 @@ def tile_simplifiedretnet_pa_kernel(tc, q, k, v, decay, out):
         outputs(0, 3, 1, "scalar")
         table(1, 1, 2)
         table(1, 1, 3)
-        quantise("s", 5)
         scores(1, 0, 2)
+        quantise("s", 5)
         scores(1, 1, 2)
-        quantise("s", 6)
         outputs(1, 0, 0, "scalar")
         outputs(1, 0, 1, "scalar")
         scores(1, 0, 3)
+        quantise("s", 6)
         scores(1, 1, 3)
-        quantise("s", 7)
         outputs(1, 1, 0, "scalar")
         outputs(1, 1, 1, "scalar")
+        quantise("s", 7)
         outputs(1, 2, 0, "scalar")
         outputs(1, 2, 1, "vector")
         outputs(1, 3, 0, "vector")

@@ -82,6 +82,8 @@ def tile_simplifiedretnet_pa_kernel(tc, q, k, v, decay, out):
                 nc.vector.tensor_copy(out=dst, in_=src)
             else:
                 nc.scalar.copy(out=dst, in_=src)
+            if n < 6:
+                keep_busy(1, BANK // 2)
 
         def quantise(kind, n):
             width = grouped[(kind, n)].shape[1]
@@ -136,6 +138,14 @@ def tile_simplifiedretnet_pa_kernel(tc, q, k, v, decay, out):
             row = CHUNK * c + P * a
             nc.sync.dma_start(out=out2[row : row + P, BANK * hh : BANK * (hh + 1)], in_=stages[(c, a, hh)][:])
 
+        def keep_busy(count, width):
+            bank = psum.tile([P, BANK], F32, name="bank")
+            for i in range(count):
+                nc.tensor.matmul(out=bank[:, 0:width], lhsT=spin[:, 0:P], rhs=spin[:, 0:width], start=True, stop=True)
+
+        spin = keep.tile([P, BANK], BF16, name="spin")
+        nc.vector.memset(spin[:].bitcast(I32), 0)
+        keep_busy(6, BANK)
         dec = keep.tile([P, 2 * TILES], BF16, name="dec")
         with nc.allow_non_contiguous_dma(reason="1024 decay rates, one key to a partition"):
             nc.scalar.dma_start(out=dec[:], in_=decay.rearrange("(t p) -> p t", p=P))

@@ -224,6 +224,7 @@ def tile_simplifiedretnet_pa_kernel(tc, q, k, v, decay, out):
             quantise("q", n)
             quantise("k", n)
 
+        keep_busy(4, BANK)
         outputs(0, 0, 0, "scalar")
         outputs(0, 0, 1, "scalar")
         scores(1, 0, 0)

from contextlib import ExitStack

import concourse.mybir as mybir
from concourse.masks import make_identity

F32 = mybir.dt.float32
BF16 = mybir.dt.bfloat16
I32 = mybir.dt.int32
U32 = mybir.dt.uint32
U8 = mybir.dt.uint8
FP8X4 = mybir.dt.float8_e4m3fn_x4
ALU = mybir.AluOpType
ACT = mybir.ActivationFunctionType

P = 128
S = 1024
H = 1024
CHUNK = 512
TILES = CHUNK // P
BANK = 512
FLOPS = 2 * 2 * H * (CHUNK * CHUNK + CHUNK * 2 * CHUNK)


def tile_simplifiedretnet_pa_kernel(tc, q, k, v, decay, out):
    nc = tc.nc
    dram = {
        "q": q.rearrange("b s h -> (b s) h"),
        "k": k.rearrange("b s h -> (b s) h"),
        "v": v.rearrange("b s h -> (b s) h"),
    }
    out2 = out.rearrange("b s h -> (b s) h")

    with ExitStack() as stack:
        keep = stack.enter_context(tc.tile_pool(name="keep", bufs=1))
        psum = stack.enter_context(tc.psum_pool(name="psum", bufs=8))
        stack.enter_context(tc.manual_schedule())

        raw = {}
        grouped = {}
        banks = {}
        codes = {}
        planes = {}
        tables = {}
        stages = {}

        def load_rows(kind, n):
            raw[(kind, n)] = keep.tile([P, H], BF16, name="raw_%s%d" % (kind, n))
            nc.sync.dma_start(out=raw[(kind, n)][:], in_=dram[kind][P * n : P * (n + 1), :])

        def load_values(g):
            raw[("v", g)] = keep.tile([P, TILES * H], BF16, name="raw_v%d" % g)
            view = raw[("v", g)][:].rearrange("p (t h) -> p t h", t=TILES)
            rows = dram["v"][CHUNK * g : CHUNK * (g + 1), :].rearrange("(t p) h -> p t h", p=P)
            for half in range(2):
                nc.sync.dma_start(out=view[:, 2 * half : 2 * half + 2, :], in_=rows[:, 2 * half : 2 * half + 2, :])

        def table(c, g, t):
            if (c, g) not in tables:
                tables[(c, g)] = keep.tile([P, TILES * CHUNK], F32, name="m%d%d" % (c, g))
            i0 = P * t if g == c else 0
            y0 = 0 if g == c else CHUNK - P * t
            m = tables[(c, g)]
            nc.scalar.activation(
                out=m[:, CHUNK * t + i0 : CHUNK * (t + 1)], in_=dist[:, y0 : y0 + CHUNK - i0], func=ACT.Exp,
                scale=negd[:, TILES * g + t : TILES * g + t + 1],
            )
            if g == c:
                corner = m[:, CHUNK * t + i0 : CHUNK * t + i0 + P]
                nc.gpsimd.affine_select(
                    out=corner, in_=corner, pattern=[[1, P]], compare_op=ALU.is_ge, fill=0.0, base=0, channel_multiplier=-1
                )

        def flip(kind, n, engine):
            words = raw[(kind, n)][:].bitcast(F32)
            bank = psum.tile([P, BANK], F32, name="bank")
            for w in range(4):
                nc.tensor.transpose(bank[:, P * w : P * (w + 1)], words[:, P * w : P * (w + 1)], ident[:])
            grouped[(kind, n)] = keep.tile([P, H], BF16, name="g_%s%d" % (kind, n), align_bytes=64)
            dst = grouped[(kind, n)][:].bitcast(F32).rearrange("p (g r u) -> p g r u", g=2, u=2)
            src = bank[:].rearrange("p (g u r) -> p g r u", g=2, u=2)
            if engine == "vector":
                nc.vector.tensor_copy(out=dst, in_=src)
            else:
                nc.scalar.copy(out=dst, in_=src)
            if n < 6:
                keep_busy(1, BANK // 2)

        def quantise(kind, n):
            width = grouped[(kind, n)].shape[1]
            cd = keep.tile([P, width // 4], U32, name="c_%s%d" % (kind, n), align_bytes=64)
            pl = keep.tile([P, width // 4], U8, name="p_%s%d" % (kind, n), align_bytes=64)
            nc.vector.quantize_mx(out=cd[:].bitcast(FP8X4), scales=pl[:], in_=grouped[(kind, n)][:])
            codes[(kind, n)] = cd
            planes[(kind, n)] = pl

        def regroup_values(g, hh):
            grouped[("v", 2 * g + hh)] = keep.tile([P, 4 * BANK], BF16, name="g_v%d%d" % (g, hh), align_bytes=64)
            src = raw[("v", g)][:].rearrange("p (t h) -> p t h", t=TILES)[:, :, BANK * hh : BANK * (hh + 1)]
            nc.vector.tensor_copy(
                out=grouped[("v", 2 * g + hh)][:].rearrange("p (c i t) -> p c t i", i=4, t=4),
                in_=src.rearrange("p t (c i) -> p c t i", i=4),
            )

        def mx(dst, left, lcols, right, rcols, start, stop):
            nc.tensor.matmul_mx(
                out=dst,
                lhsT=codes[left][:, lcols].bitcast(FP8X4), lhsT_scale=planes[left][:, lcols],
                rhs=codes[right][:, rcols].bitcast(FP8X4), rhs_scale=planes[right][:, rcols],
                start=start, stop=stop,
            )

        def scores(c, g, a):
            nt = TILES if g < c else a + 1
            bank = psum.tile([P, BANK], F32, name="bank")
            for t in range(nt):
                for hp in range(2):
                    cols = slice(P * hp, P * (hp + 1))
                    mx(bank[:, P * t : P * (t + 1)], ("k", TILES * g + t), cols, ("q", TILES * c + a), cols, hp == 0, hp == 1)
            m = tables[(c, g)][:].rearrange("p (t i) -> p t i", t=TILES)
            part = grouped[("s", TILES * c + a)][:, CHUNK * g : CHUNK * (g + 1)]
            nc.vector.scalar_tensor_tensor(
                out=part.rearrange("p (i t) -> p i t", t=TILES)[:, :, 0:nt],
                in0=bank[:].rearrange("p (t i) -> p i t", t=TILES)[:, :, 0:nt],
                scalar=1.0 / 32.0,
                in1=m[:, 0:nt, P * a : P * (a + 1)].rearrange("p t i -> p i t"),
                op0=ALU.mult, op1=ALU.mult,
            )

        def outputs(c, a, hh, engine):
            acc = psum.tile([P, BANK], F32, name="bank")
            for g in range(c + 1):
                mx(acc[:], ("s", TILES * c + a), slice(P * g, P * (g + 1)), ("v", 2 * g + hh), slice(0, BANK), g == 0, g == c)
            stages[(c, a, hh)] = keep.tile([P, BANK], F32, name="o%d%d%d" % (c, a, hh))
            if engine == "vector":
                nc.vector.tensor_copy(out=stages[(c, a, hh)][:], in_=acc[:])
            else:
                nc.scalar.copy(out=stages[(c, a, hh)][:], in_=acc[:])
            row = CHUNK * c + P * a
            nc.sync.dma_start(out=out2[row : row + P, BANK * hh : BANK * (hh + 1)], in_=stages[(c, a, hh)][:])

        def keep_busy(count, width):
            bank = psum.tile([P, BANK], F32, name="bank")
            for i in range(count):
                nc.tensor.matmul(out=bank[:, 0:width], lhsT=spin[:, 0:P], rhs=spin[:, 0:width], start=True, stop=True)

        spin = keep.tile([P, BANK], BF16, name="spin")
        nc.vector.memset(spin[:].bitcast(I32), 0)
        keep_busy(6, BANK)
        dec = keep.tile([P, 2 * TILES], BF16, name="dec")
        with nc.allow_non_contiguous_dma(reason="1024 decay rates, one key to a partition"):
            nc.scalar.dma_start(out=dec[:], in_=decay.rearrange("(t p) -> p t", p=P))
        for n in range(TILES):
            load_rows("k", n)
            load_rows("q", n)
        load_values(0)
        for n in range(TILES, 2 * TILES):
            load_rows("q", n)
            load_rows("k", n)
        load_values(1)

        warm = keep.tile([P, 1], F32, name="warm")
        nc.vector.memset(warm[:], 0.0)
        warm2 = keep.tile([P, 1], F32, name="warm2")
        nc.scalar.activation(out=warm2[:], in_=warm[:], func=ACT.Exp)
        ident = keep.tile([P, P], F32, name="ident")
        make_identity(nc, ident[:])
        ramp = keep.tile([P, 256], I32, name="ramp")
        nc.gpsimd.iota(ramp[:], pattern=[[1, 256]], base=0, channel_multiplier=-1)
        for c in range(2):
            for a in range(TILES):
                n = TILES * c + a
                grouped[("s", n)] = keep.tile([P, (c + 1) * CHUNK], BF16, name="g_s%d" % n, align_bytes=64)
                if a < TILES - 1:
                    nc.vector.memset(grouped[("s", n)][:, c * CHUNK : (c + 1) * CHUNK], 0.0)
        dist = keep.tile([P, S], F32, name="dist")
        for b in range(4):
            nc.vector.tensor_scalar(
                out=dist[:, 256 * b : 256 * (b + 1)], in0=ramp[:], scalar1=float(256 * b), scalar2=0.0,
                op0=ALU.add, op1=ALU.max,
            )
        negd = keep.tile([P, 2 * TILES], F32, name="negd")
        nc.vector.tensor_scalar_mul(out=negd[:], in0=dec[:], scalar1=-1.0)

        flip("k", 0, "vector")
        table(0, 0, 0)
        table(0, 0, 1)
        flip("q", 0, "vector")
        flip("k", 1, "vector")
        table(0, 0, 2)
        flip("q", 1, "scalar")
        for n in range(2):
            quantise("k", n)
            quantise("q", n)
        flip("k", 2, "scalar")
        flip("q", 2, "scalar")
        scores(0, 0, 0)
        quantise("k", 2)
        quantise("q", 2)
        flip("k", 3, "scalar")
        flip("q", 3, "scalar")
        table(0, 0, 3)
        scores(0, 0, 1)
        quantise("s", 0)
        quantise("k", 3)
        quantise("q", 3)
        scores(0, 0, 2)
        quantise("s", 1)
        table(1, 0, 0)
        table(1, 0, 1)
        regroup_values(0, 0)
        scores(0, 0, 3)
        regroup_values(0, 1)
        for n in (4, 5):
            flip("q", n, "scalar")
            flip("k", n, "scalar")
        quantise("s", 2)
        quantise("v", 0)
        quantise("s", 3)
        quantise("v", 1)
        table(1, 0, 2)
        table(1, 0, 3)
        table(1, 1, 0)
        for n in (4, 5):
            quantise("q", n)
            quantise("k", n)

        keep_busy(4, BANK)
        outputs(0, 0, 0, "scalar")
        outputs(0, 0, 1, "scalar")
        scores(1, 0, 0)
        scores(1, 1, 0)
        outputs(0, 1, 0, "scalar")
        outputs(0, 1, 1, "scalar")
        regroup_values(1, 0)
        regroup_values(1, 1)
        for n in (6, 7):
            flip("q", n, "scalar")
            flip("k", n, "scalar")
        table(1, 1, 1)
        quantise("s", 4)
        for n in (6, 7):
            quantise("q", n)
            quantise("k", n)
        quantise("v", 2)
        quantise("v", 3)
        outputs(0, 2, 0, "scalar")
        outputs(0, 2, 1, "scalar")
        scores(1, 0, 1)
        scores(1, 1, 1)
        outputs(0, 3, 0, "scalar")
        outputs(0, 3, 1, "scalar")
        table(1, 1, 2)
        table(1, 1, 3)
        scores(1, 0, 2)
        quantise("s", 5)
        scores(1, 1, 2)
        outputs(1, 0, 0, "scalar")
        outputs(1, 0, 1, "scalar")
        scores(1, 0, 3)
        quantise("s", 6)
        scores(1, 1, 3)
        outputs(1, 1, 0, "scalar")
        outputs(1, 1, 1, "scalar")
        quantise("s", 7)
        outputs(1, 2, 0, "scalar")
        outputs(1, 2, 1, "vector")
        outputs(1, 3, 0, "vector")
        outputs(1, 3, 1, "scalar")
